import numpy as np
import ml_dtypes


def mxq(x, axis, fmt="e4m3"):
    dtype, down = {"e4m3": (ml_dtypes.float8_e4m3fn, 7), "e5m2": (ml_dtypes.float8_e5m2, 14)}[fmt]
    v = np.moveaxis(np.asarray(x, np.float32).astype(ml_dtypes.bfloat16).astype(np.float64), axis, -1)
    blocks = v.reshape(v.shape[:-1] + (-1, 32))
    amax = np.abs(blocks).max(-1, keepdims=True)
    byte = np.maximum(np.where(amax > 0, np.frexp(amax)[1] - 1 + 127, 0) - down, 1)
    scale = np.exp2(byte - 127.0)
    codes = (blocks / scale).astype(np.float32).astype(dtype).astype(np.float64)
    return np.moveaxis((codes * scale).reshape(v.shape), -1, axis)


WIDE = False


def mx_kscale(k):
    if not WIDE:
        return np.ones(k)
    levels = np.array([10, -10, 5, -5, 0])
    if k % 512:
        return np.exp2(np.random.permutation(np.resize(levels, k // 32))).repeat(32)
    a = np.empty((k // 512, 16))
    for p in range(k // 512):
        a[p, :8] = np.random.permutation(np.resize(levels, 8))
        for g in range(8):
            far = levels[np.abs(levels - a[p, g]) >= 10]
            a[p, g + 8] = far[np.random.randint(len(far))]
    return np.exp2(a.ravel()).repeat(32)


BF16 = ml_dtypes.bfloat16


def bf(x):
    return np.asarray(x, np.float32).astype(BF16)


def f64(x):
    return np.asarray(x).astype(np.float64)


B, T, C, CO, HS, DW, DA, DV, DG = 4, 128, 2048, 2048, 64, 128, 128, 128, 256
H = C // HS
EPS_GN = 0.00064


def setup_inputs():
    n = np.random.standard_normal
    t = mx_kscale(C)
    return {
        "y": bf(n((B, T, C)) * 0.1),
        "r": bf(n((B, T, C))),
        "k": bf(n((B, T, C)) * 0.6),
        "v": bf(n((B, T, C)) * 0.8),
        "g_hid": bf(1.0 / (1.0 + np.exp(-n((B, T, DG))))),
        "g2": bf(n((DG, C)) * 2.0 / np.sqrt(DG) * t),
        "r_k": bf(n((H, HS)) * 0.2 - 0.04),
        "ln_g": bf(1.0 + n((C,)) * 0.1),
        "ln_b": bf(n((C,)) * 0.1),
        "W_o": bf(n((CO, C)) * 0.7 / np.sqrt(C) / t),
    }


def reference(y, r, k, v, g_hid, g2, r_k, ln_g, ln_b, W_o):
    yh = f64(y).reshape(B, T, H, HS)
    mu = np.mean(yh, axis=-1, keepdims=True)
    var = np.mean((yh - mu) ** 2, axis=-1, keepdims=True)
    yn = ((yh - mu) / np.sqrt(var + EPS_GN)).reshape(B, T, C)
    yn = yn * f64(ln_g) + f64(ln_b)
    rh = f64(r).reshape(B, T, H, HS)
    kh = f64(k).reshape(B, T, H, HS)
    vh = f64(v).reshape(B, T, H, HS)
    dot = np.sum(rh * kh * f64(r_k), axis=-1, keepdims=True)
    y2 = yn + (dot * vh).reshape(B, T, C)
    g = f64(g_hid) @ f64(g2)
    z = y2 * g
    return mxq(z, 2, "e4m3") @ mxq(f64(W_o), 1, "e4m3").T

@@ -1,0 +1,329 @@
+from contextlib import ExitStack
+
+import concourse.mybir as mybir
+from concourse.masks import make_identity
+
+F32 = mybir.dt.float32
+BF16 = mybir.dt.bfloat16
+U32 = mybir.dt.uint32
+U8 = mybir.dt.uint8
+FP8X4 = mybir.dt.float8_e4m3fn_x4
+ADD = mybir.AluOpType.add
+SUB = mybir.AluOpType.subtract
+MUL = mybir.AluOpType.mult
+IDENTITY = mybir.ActivationFunctionType.Identity
+COPY = mybir.ActivationFunctionType.Copy
+SQRT = mybir.ActivationFunctionType.Sqrt
+AXIS_X = mybir.AxisListType.X
+
+P = 128
+TILES = 4
+C = 2048
+CO = 2048
+HEAD = 64
+HEADS = C // HEAD
+PASSES = 4
+UNITS = TILES * PASSES
+PAIRS = 8
+EPS = 0.00064
+GW = 256
+
+FLOPS = 2 * 512 * 2048 * 2048 + 2 * 512 * 256 * 2048
+
+
+def tile_full_tmix_params_pc_kernel(tc, y, r, k, v, g_hid, g2, r_k, ln_g, ln_b, W_o, out):
+    nc = tc.nc
+    with ExitStack() as ctx:
+        const = ctx.enter_context(tc.tile_pool(name="const", bufs=1))
+        ld = ctx.enter_context(tc.tile_pool(name="ld", bufs=22))
+        work = ctx.enter_context(tc.tile_pool(name="work", bufs=2))
+        psum = ctx.enter_context(tc.psum_pool(name="psum", bufs=1))
+        ctx.enter_context(tc.manual_schedule())
+
+        ident = const.tile([P, P], F32, name="ident")
+        make_identity(nc, ident[:])
+        rk_row = ld.tile([P, C], BF16, name="rk_row", tag="ld")
+        nc.vector.memset(rk_row[:], 0.0)
+        ln_rows = const.tile([P, 4 * P], BF16, name="ln_rows")
+        nc.vector.memset(ln_rows[:], 0.0)
+        ones = const.tile([P, P], BF16, name="ones")
+        nc.vector.memset(ones[:], 1.0)
+        gh_rows = const.tile([P, TILES * 256], BF16, name="gh_rows")
+        g2_sb = const.tile([P, 2, C], BF16, name="g2_sb")
+
+        y_sb, r_sb, k_sb, v_sb, w_sb = {}, {}, {}, {}, {}
+
+        def load(src, label):
+            t = ld.tile([P, C], BF16, name=label, tag="ld")
+            nc.sync.dma_start(out=t[:], in_=src)
+            return t
+
+        def load_y(m):
+            y_sb[m] = load(y[m], "y%d" % m)
+
+        def load_rk(m):
+            r_sb[m] = load(r[m], "r%d" % m)
+            k_sb[m] = load(k[m], "k%d" % m)
+
+        def load_v(m):
+            v_sb[m] = load(v[m], "v%d" % m)
+
+        def load_w(pair):
+            for b in range(2):
+                row = 256 * pair + P * b
+                w_sb[(pair, b)] = load(W_o[row:row + P, :], "w%d_%d" % (pair, b))
+
+        load_y(0)
+        nc.sync.dma_start(out=rk_row[0:1, :], in_=r_k.rearrange("(o h) i -> o (h i)", o=1))
+        nc.sync.dma_start(out=gh_rows[:].rearrange("t (b d) -> t b d", b=TILES), in_=g_hid.rearrange("b t d -> t b d"))
+        nc.sync.dma_start(out=ln_rows[0:4, :], in_=ln_g.rearrange("(a b) -> a b", b=4 * P))
+        nc.sync.dma_start(out=ln_rows[4:8, :], in_=ln_b.rearrange("(a b) -> a b", b=4 * P))
+        load_rk(0)
+        load_w(0)
+        load_w(1)
+        load_w(2)
+        load_w(3)
+        load_y(1)
+        load_rk(1)
+        load_w(4)
+        load_w(5)
+        load_v(0)
+        load_w(6)
+        for e in range(2):
+            nc.sync.dma_start(out=g2_sb[:, e, :], in_=g2.rearrange("(q e) c -> e q c", e=2)[e])
+        load_w(7)
+        load_y(2)
+        load_rk(2)
+        load_v(1)
+        load_y(3)
+        load_rk(3)
+        load_v(2)
+        load_v(3)
+
+        rk_all = const.tile([P, C], BF16, name="rk_all")
+        ln_words = const.tile([P, 16], F32, name="ln_words")
+        ln_cols = const.tile([P, 32], F32, name="ln_cols")
+        gh_t = const.tile([P, 2, 512], BF16, name="gh_t")
+        w_codes = const.tile([P, PASSES, CO], U32, name="w_codes", align_bytes=64)
+        w_scales = const.tile([P, PASSES, CO], U8, name="w_scales", align_bytes=64)
+        z_codes = const.tile([P, TILES, 512], U32, name="z_codes", align_bytes=64)
+        z_scales = const.tile([P, TILES, 512], U8, name="z_scales", align_bytes=64)
+
+        def spread_r_k():
+            for j in range(4):
+                acc = psum.tile([P, 512], F32, name="rk_ps%d" % j, tag=("A", "B", "G", "X")[j], bufs=(1, 1, 1, 5)[j])
+                nc.tensor.matmul(acc[:], lhsT=ones[:], rhs=rk_row[:, 512 * j:512 * j + 512], start=True, stop=True)
+                nc.scalar.copy(out=rk_all[:, 512 * j:512 * j + 512], in_=acc[:])
+
+        def turn_ln_and_g_hid():
+            ln_ps = psum.tile([P, 2, P], F32, name="ln_ps", tag="B", bufs=1)
+            for half in range(2):
+                nc.tensor.transpose(ln_ps[:, half, :], ln_rows[:].bitcast(F32)[:, half:2 * P:2], ident[:])
+            nc.vector.tensor_copy(out=ln_words[:].rearrange("p (n u) -> p n u", u=2), in_=ln_ps[:, :, 0:8].rearrange("p u n -> p n u"))
+            nc.vector.tensor_copy(out=ln_cols[:], in_=ln_words[:].bitcast(BF16))
+            gh_ps = psum.tile([P, 512], F32, name="gh_ps", tag="G", bufs=1)
+            for m in range(TILES):
+                nc.tensor.transpose(gh_ps[:, P * m:P * m + P], gh_rows[:].bitcast(F32)[:, P * m:P * m + P], ident[:])
+            nc.vector.tensor_copy(out=gh_t[:], in_=gh_ps[:].bitcast(BF16).rearrange("q (n e) -> q e n", e=2))
+
+        bn_out, sums, var_eps, std, a_b, dots, rkw = {}, {}, {}, {}, {}, {}, {}
+        s1, s2, s1_ps, s2_ps, gate_ps, e1, z_bf, w_bf, w_ps, out_ps = {}, {}, {}, {}, {}, {}, {}, {}, {}, {}
+
+        def bn_part(m, part):
+            if part == 0:
+                bn_out[m] = work.tile([P, HEADS, 6], F32, name="bn%d" % m, tag="bn")
+            for h in range(8 * part, 8 * part + 8):
+                nc.vector.bn_stats(out=bn_out[m][:, h, :], in_=y_sb[m][:, HEAD * h:HEAD * h + HEAD])
+
+        def variance(m):
+            st = bn_out[m]
+            sums[m] = work.tile([P, HEADS, 2], F32, name="sums%d" % m, tag="sums")
+            nc.vector.tensor_tensor(out=sums[m][:], in0=st[:, :, 1:3], in1=st[:, :, 4:6], op=ADD)
+            diff = work.tile([P, HEADS], F32, name="diff%d" % m, tag="diff")
+            nc.vector.tensor_tensor(out=diff[:], in0=st[:, :, 1], in1=st[:, :, 4], op=SUB)
+            within = work.tile([P, HEADS], F32, name="within%d" % m, tag="within")
+            nc.vector.tensor_scalar(out=within[:], in0=sums[m][:, :, 1], scalar1=1.0 / HEAD, scalar2=EPS, op0=MUL, op1=ADD)
+            diff2 = work.tile([P, HEADS], F32, name="diffsq%d" % m, tag="diffsq")
+            nc.vector.tensor_tensor(out=diff2[:], in0=diff[:], in1=diff[:], op=MUL)
+            var_eps[m] = work.tile([P, HEADS], F32, name="vareps%d" % m, tag="vareps")
+            nc.vector.scalar_tensor_tensor(out=var_eps[m][:], in0=diff2[:], scalar=0.25, in1=within[:], op0=MUL, op1=ADD)
+
+        def root(m):
+            std[m] = work.tile([P, HEADS], F32, name="std%d" % m, tag="std")
+            nc.scalar.activation(out=std[m][:], in_=var_eps[m][:], func=SQRT)
+
+        def scale_and_shift(m):
+            a_b[m] = work.tile([P, 2, HEADS], F32, name="ab%d" % m, tag="ab")
+            nc.vector.reciprocal(out=a_b[m][:, 0, :], in_=std[m][:])
+            nc.vector.scalar_tensor_tensor(out=a_b[m][:, 1, :], in0=sums[m][:, :, 0], scalar=-0.5, in1=a_b[m][:, 0, :],
+                                           op0=MUL, op1=MUL)
+
+        def products(m):
+            rkw[m] = work.tile([P, C], F32, name="rkw%d" % m, tag="rkw")
+            dots[m] = work.tile([P, HEADS], F32, name="dot%d" % m, tag="dot")
+            for first in range(0, C, 2 * GW):
+                both = (slice(first, first + GW), slice(first + GW, first + 2 * GW))
+                for cols in both:
+                    nc.gpsimd.tensor_tensor(out=rkw[m][:, cols], in0=r_sb[m][:, cols], in1=k_sb[m][:, cols], op=MUL)
+                for cols in both:
+                    nc.gpsimd.tensor_tensor(out=rkw[m][:, cols], in0=rkw[m][:, cols], in1=rk_all[:, cols], op=MUL)
+
+        def dot_sum(m, g):
+            nc.vector.tensor_reduce(out=dots[m][:, 8 * g:8 * g + 8],
+                                    in_=rkw[m][:, 512 * g:512 * g + 512].rearrange("t (h i) -> t h i", i=HEAD),
+                                    axis=AXIS_X, op=ADD)
+
+        def split_view(tile_ap, h):
+            return tile_ap[:, HEAD * h:HEAD * h + HEAD].rearrange("t (p f) -> t f p", f=4)
+
+        def norm_heads(u):
+            m, g = divmod(u, PASSES)
+            s1[u] = work.tile([P, 4, P], F32, name="s1_%d" % u, tag="s1", bufs=3)
+            for i in range(8):
+                h = 8 * g + i
+                nc.scalar.activation(out=s1[u][:, :, 16 * i:16 * i + 16],
+                                     in_=split_view(y_sb[m], h), func=IDENTITY,
+                                     bias=a_b[m][:, 1, h:h + 1], scale=a_b[m][:, 0, h:h + 1])
+
+        def bonus_heads(u):
+            m, g = divmod(u, PASSES)
+            s2[u] = work.tile([P, 4, P], F32, name="s2_%d" % u, tag="s2", bufs=3)
+            for i in range(8):
+                h = 8 * g + i
+                nc.scalar.activation(out=s2[u][:, :, 16 * i:16 * i + 16],
+                                     in_=split_view(v_sb[m], h), func=COPY, scale=dots[m][:, h:h + 1])
+
+        def turn_s1(u):
+            s1_ps[u] = psum.tile([P, 4, P], F32, name="s1ps%d" % u, tag="A", bufs=1)
+            for t in range(4):
+                nc.tensor.transpose(s1_ps[u][:, t, :], s1[u][:, t, :], ident[:])
+
+        def turn_s2(u):
+            s2_ps[u] = psum.tile([P, 4, P], F32, name="s2ps%d" % u, tag="B", bufs=1)
+            for t in range(4):
+                nc.tensor.transpose(s2_ps[u][:, t, :], s2[u][:, t, :], ident[:])
+
+        def gate(u):
+            m, g = divmod(u, PASSES)
+            gate_ps[u] = psum.tile([P, 4, P], F32, name="gps%d" % u, tag="G", bufs=1)
+            for t in range(4):
+                for e in range(2):
+                    every_fourth = g2_sb[:, e, 512 * g:512 * g + 512].rearrange("q (p f) -> q f p", f=4)[:, t, :]
+                    nc.tensor.matmul(gate_ps[u][:, t, :], lhsT=every_fourth, rhs=gh_t[:, e, P * m:P * m + P],
+                                     start=(e == 0), stop=(e == 1))
+
+        def gain_and_bias(u):
+            g = u % PASSES
+            e1[u] = work.tile([P, 4, P], F32, name="e1_%d" % u, tag="e1", bufs=3)
+            for t in range(4):
+                blk = 4 * g + t
+                nc.scalar.activation(out=e1[u][:, t, :], in_=s1_ps[u][:, t, :], func=IDENTITY,
+                                     bias=ln_cols[:, 16 + blk:17 + blk], scale=ln_cols[:, blk:blk + 1])
+
+        def add_bonus(u):
+            nc.vector.tensor_tensor(out=e1[u][:], in0=e1[u][:], in1=s2_ps[u][:], op=ADD)
+
+        def times_gate(u):
+            z_bf[u] = work.tile([P, P, 4], BF16, name="z%d" % u, tag="z", bufs=3, align_bytes=64)
+            nc.vector.tensor_tensor(out=z_bf[u][:], in0=e1[u][:].rearrange("p t r -> p r t"),
+                                    in1=gate_ps[u][:].rearrange("p t r -> p r t"), op=MUL)
+
+        def quantise_z(u):
+            m, g = divmod(u, PASSES)
+            nc.vector.quantize_mx(out=z_codes[:, m, P * g:P * g + P].bitcast(FP8X4), scales=z_scales[:, m, P * g:P * g + P],
+                                  in_=z_bf[u][:].rearrange("p r t -> p (r t)"))
+
+        def turn_w(pair):
+            for g in range(PASSES):
+                w_ps[(pair, g)] = psum.tile([P, 2, 256], F32, name="wps%d_%d" % (pair, g), tag="X", bufs=5)
+                for half in range(2):
+                    for b in range(2):
+                        nc.tensor.transpose(w_ps[(pair, g)][:, half, P * b:P * b + P],
+                                            w_sb[(pair, b)][:].bitcast(F32)[:, 256 * g + half:256 * g + 256:2], ident[:])
+
+        def regroup_w(pair):
+            w_bf[pair] = work.tile([P, 4096], BF16, name="wbf%d" % pair, tag="wbf", bufs=2, align_bytes=64)
+            words = w_bf[pair][:].bitcast(F32).rearrange("p (g c u) -> p g c u", g=PASSES, u=2)
+            for g in range(PASSES):
+                nc.scalar.copy(out=words[:, g, :, :], in_=w_ps[(pair, g)][:].rearrange("p u c -> p c u"))
+
+        def quantise_w(pair, passes):
+            for g in passes:
+                nc.vector.quantize_mx(out=w_codes[:, g, 256 * pair:256 * pair + 256].bitcast(FP8X4),
+                                      scales=w_scales[:, g, 256 * pair:256 * pair + 256],
+                                      in_=w_bf[pair][:, 1024 * g:1024 * g + 1024])
+
+        def mx_passes(u):
+            m, g = divmod(u, PASSES)
+            for n in range(4):
+                if g == 0:
+                    out_ps[(m, n)] = psum.tile([P, 512], F32, name="ops%d_%d" % (m, n), tag="X", bufs=5)
+                nc.tensor.matmul_mx(out=out_ps[(m, n)][:],
+                                    lhsT=z_codes[:, m, P * g:P * g + P].bitcast(FP8X4), lhsT_scale=z_scales[:, m, P * g:P * g + P],
+                                    rhs=w_codes[:, g, 512 * n:512 * n + 512].bitcast(FP8X4), rhs_scale=w_scales[:, g, 512 * n:512 * n + 512],
+                                    start=(g == 0), stop=(g == PASSES - 1))
+
+        def store_tile(m):
+            for n in range(4):
+                res = work.tile([P, 512], F32, name="res%d_%d" % (m, n), tag="res", bufs=4)
+                if m == TILES - 1 and n % 2 == 1:
+                    nc.vector.tensor_copy(out=res[:], in_=out_ps[(m, n)][:])
+                else:
+                    nc.scalar.copy(out=res[:], in_=out_ps[(m, n)][:])
+                nc.sync.dma_start(out=out[m, :, 512 * n:512 * n + 512], in_=res[:])
+
+        def is_unit(u):
+            return 0 <= u < UNITS
+
+        spread_r_k()
+        for s in range(-9, UNITS + 1):
+            token = [(m, s - (5 * m - 9)) for m in range(TILES) if 0 <= s - (5 * m - 9) < 6]
+            done_pair = s + 7
+            if is_unit(s):
+                add_bonus(s)
+            for (m, t) in token:
+                if t < 2:
+                    bn_part(m, 2 * t)
+                if t == 3:
+                    scale_and_shift(m)
+                if t == 0:
+                    products(m)
+            if 0 <= done_pair < PAIRS:
+                quantise_w(done_pair, (0, 1))
+            if is_unit(s):
+                times_gate(s)
+            for (m, t) in token:
+                if t < 2:
+                    bn_part(m, 2 * t + 1)
+                if t == 1:
+                    variance(m)
+            if 0 <= done_pair < PAIRS:
+                quantise_w(done_pair, (2, 3))
+            if is_unit(s):
+                quantise_z(s)
+            for (m, t) in token:
+                if t >= 2:
+                    dot_sum(m, t - 2)
+            if s == -8:
+                turn_ln_and_g_hid()
+            if 0 <= s + 8 < PAIRS:
+                turn_w(s + 8)
+            if is_unit(s + 1):
+                turn_s2(s + 1)
+                gate(s + 1)
+            if is_unit(s + 2):
+                turn_s1(s + 2)
+            if is_unit(s - 1):
+                mx_passes(s - 1)
+            for (m, t) in token:
+                if t == 2:
+                    root(m)
+            if 0 <= s + 8 < PAIRS:
+                regroup_w(s + 8)
+            if is_unit(s + 2):
+                bonus_heads(s + 2)
+                gain_and_bias(s + 2)
+            if is_unit(s + 3):
+                norm_heads(s + 3)
+            if s >= PASSES and s % PASSES == 0:
+                store_tile(s // PASSES - 1)

@@ -35,7 +35,7 @@ def tile_full_tmix_params_pc_kernel(tc, y, r, k, v, g_hid, g2, r_k, ln_g, ln_b, 
     nc = tc.nc
     with ExitStack() as ctx:
         const = ctx.enter_context(tc.tile_pool(name="const", bufs=1))
-        ld = ctx.enter_context(tc.tile_pool(name="ld", bufs=22))
+        ld = ctx.enter_context(tc.tile_pool(name="ld", bufs=26))
         work = ctx.enter_context(tc.tile_pool(name="work", bufs=2))
         psum = ctx.enter_context(tc.psum_pool(name="psum", bufs=1))
         ctx.enter_context(tc.manual_schedule())
@@ -43,9 +43,9 @@ def tile_full_tmix_params_pc_kernel(tc, y, r, k, v, g_hid, g2, r_k, ln_g, ln_b, 
         ident = const.tile([P, P], F32, name="ident")
         make_identity(nc, ident[:])
         rk_row = ld.tile([P, C], BF16, name="rk_row", tag="ld")
-        nc.vector.memset(rk_row[:], 0.0)
+        nc.vector.memset(rk_row[:].bitcast(U32), 0)
         ln_rows = const.tile([P, 4 * P], BF16, name="ln_rows")
-        nc.vector.memset(ln_rows[:], 0.0)
+        nc.vector.memset(ln_rows[:].bitcast(U32), 0)
         ones = const.tile([P, P], BF16, name="ones")
         nc.vector.memset(ones[:], 1.0)
         gh_rows = const.tile([P, TILES * 256], BF16, name="gh_rows")
@@ -75,29 +75,29 @@ def tile_full_tmix_params_pc_kernel(tc, y, r, k, v, g_hid, g2, r_k, ln_g, ln_b, 
 
         load_y(0)
         nc.sync.dma_start(out=rk_row[0:1, :], in_=r_k.rearrange("(o h) i -> o (h i)", o=1))
+        load_rk(0)
         nc.sync.dma_start(out=gh_rows[:].rearrange("t (b d) -> t b d", b=TILES), in_=g_hid.rearrange("b t d -> t b d"))
         nc.sync.dma_start(out=ln_rows[0:4, :], in_=ln_g.rearrange("(a b) -> a b", b=4 * P))
         nc.sync.dma_start(out=ln_rows[4:8, :], in_=ln_b.rearrange("(a b) -> a b", b=4 * P))
-        load_rk(0)
-        load_w(0)
-        load_w(1)
-        load_w(2)
-        load_w(3)
-        load_y(1)
-        load_rk(1)
-        load_w(4)
-        load_w(5)
         load_v(0)
-        load_w(6)
         for e in range(2):
             nc.sync.dma_start(out=g2_sb[:, e, :], in_=g2.rearrange("(q e) c -> e q c", e=2)[e])
-        load_w(7)
+        load_y(1)
+        load_w(0)
+        load_w(1)
+        load_rk(1)
+        load_w(2)
+        load_v(1)
+        load_w(3)
         load_y(2)
         load_rk(2)
-        load_v(1)
+        load_w(4)
+        load_w(5)
+        load_w(6)
+        load_v(2)
+        load_w(7)
         load_y(3)
         load_rk(3)
-        load_v(2)
         load_v(3)
 
         rk_all = const.tile([P, C], BF16, name="rk_all")
@@ -126,7 +126,7 @@ def tile_full_tmix_params_pc_kernel(tc, y, r, k, v, g_hid, g2, r_k, ln_g, ln_b, 
                 nc.tensor.transpose(gh_ps[:, P * m:P * m + P], gh_rows[:].bitcast(F32)[:, P * m:P * m + P], ident[:])
             nc.vector.tensor_copy(out=gh_t[:], in_=gh_ps[:].bitcast(BF16).rearrange("q (n e) -> q e n", e=2))
 
-        bn_out, sums, var_eps, std, a_b, dots, rkw = {}, {}, {}, {}, {}, {}, {}
+        bn_out, sums, diff, var_eps, std, a_b, dots, rkw = {}, {}, {}, {}, {}, {}, {}, {}
         s1, s2, s1_ps, s2_ps, gate_ps, e1, z_bf, w_bf, w_ps, out_ps = {}, {}, {}, {}, {}, {}, {}, {}, {}, {}
 
         def bn_part(m, part):
@@ -135,16 +135,18 @@ def tile_full_tmix_params_pc_kernel(tc, y, r, k, v, g_hid, g2, r_k, ln_g, ln_b, 
             for h in range(8 * part, 8 * part + 8):
                 nc.vector.bn_stats(out=bn_out[m][:, h, :], in_=y_sb[m][:, HEAD * h:HEAD * h + HEAD])
 
-        def variance(m):
+        def variance_sums(m):
             st = bn_out[m]
             sums[m] = work.tile([P, HEADS, 2], F32, name="sums%d" % m, tag="sums")
             nc.vector.tensor_tensor(out=sums[m][:], in0=st[:, :, 1:3], in1=st[:, :, 4:6], op=ADD)
-            diff = work.tile([P, HEADS], F32, name="diff%d" % m, tag="diff")
-            nc.vector.tensor_tensor(out=diff[:], in0=st[:, :, 1], in1=st[:, :, 4], op=SUB)
+            diff[m] = work.tile([P, HEADS], F32, name="diff%d" % m, tag="diff")
+            nc.vector.tensor_tensor(out=diff[m][:], in0=st[:, :, 1], in1=st[:, :, 4], op=SUB)
+
+        def variance(m):
             within = work.tile([P, HEADS], F32, name="within%d" % m, tag="within")
             nc.vector.tensor_scalar(out=within[:], in0=sums[m][:, :, 1], scalar1=1.0 / HEAD, scalar2=EPS, op0=MUL, op1=ADD)
             diff2 = work.tile([P, HEADS], F32, name="diffsq%d" % m, tag="diffsq")
-            nc.vector.tensor_tensor(out=diff2[:], in0=diff[:], in1=diff[:], op=MUL)
+            nc.vector.tensor_tensor(out=diff2[:], in0=diff[m][:], in1=diff[m][:], op=MUL)
             var_eps[m] = work.tile([P, HEADS], F32, name="vareps%d" % m, tag="vareps")
             nc.vector.scalar_tensor_tensor(out=var_eps[m][:], in0=diff2[:], scalar=0.25, in1=within[:], op0=MUL, op1=ADD)
 
@@ -253,42 +255,47 @@ def tile_full_tmix_params_pc_kernel(tc, y, r, k, v, g_hid, g2, r_k, ln_g, ln_b, 
                                       scales=w_scales[:, g, 256 * pair:256 * pair + 256],
                                       in_=w_bf[pair][:, 1024 * g:1024 * g + 1024])
 
-        def mx_passes(u):
-            m, g = divmod(u, PASSES)
-            for n in range(4):
-                if g == 0:
-                    out_ps[(m, n)] = psum.tile([P, 512], F32, name="ops%d_%d" % (m, n), tag="X", bufs=5)
-                nc.tensor.matmul_mx(out=out_ps[(m, n)][:],
-                                    lhsT=z_codes[:, m, P * g:P * g + P].bitcast(FP8X4), lhsT_scale=z_scales[:, m, P * g:P * g + P],
-                                    rhs=w_codes[:, g, 512 * n:512 * n + 512].bitcast(FP8X4), rhs_scale=w_scales[:, g, 512 * n:512 * n + 512],
-                                    start=(g == 0), stop=(g == PASSES - 1))
+        def mx_pass(m, g, n):
+            nc.tensor.matmul_mx(out=out_ps[(m, n)][:],
+                                lhsT=z_codes[:, m, P * g:P * g + P].bitcast(FP8X4), lhsT_scale=z_scales[:, m, P * g:P * g + P],
+                                rhs=w_codes[:, g, 512 * n:512 * n + 512].bitcast(FP8X4), rhs_scale=w_scales[:, g, 512 * n:512 * n + 512],
+                                start=(g == 0), stop=(g == PASSES - 1))
 
-        def store_tile(m):
-            for n in range(4):
-                res = work.tile([P, 512], F32, name="res%d_%d" % (m, n), tag="res", bufs=4)
-                if m == TILES - 1 and n % 2 == 1:
-                    nc.vector.tensor_copy(out=res[:], in_=out_ps[(m, n)][:])
-                else:
-                    nc.scalar.copy(out=res[:], in_=out_ps[(m, n)][:])
-                nc.sync.dma_start(out=out[m, :, 512 * n:512 * n + 512], in_=res[:])
+        def open_bank(m, n):
+            out_ps[(m, n)] = psum.tile([P, 512], F32, name="ops%d_%d" % (m, n), tag="X", bufs=5)
+
+        def store(m, n, on_vector):
+            res = work.tile([P, 512], F32, name="res%d_%d" % (m, n), tag="res", bufs=4)
+            if on_vector:
+                nc.vector.tensor_copy(out=res[:], in_=out_ps[(m, n)][:])
+            else:
+                nc.scalar.copy(out=res[:], in_=out_ps[(m, n)][:])
+            nc.sync.dma_start(out=out[m, :, 512 * n:512 * n + 512], in_=res[:])
 
         def is_unit(u):
             return 0 <= u < UNITS
 
         spread_r_k()
-        for s in range(-9, UNITS + 1):
-            token = [(m, s - (5 * m - 9)) for m in range(TILES) if 0 <= s - (5 * m - 9) < 6]
-            done_pair = s + 7
+        for s in range(-6, UNITS + 1):
+            token = [(m, s - (4 * m - 6)) for m in range(TILES) if 0 <= s - (4 * m - 6) < 6]
+            done_pair = s
+            has_pair = 0 <= done_pair < PAIRS
+            group = divmod(s - 4, 4)
+            has_group = 0 <= group[0] < TILES - 1
+            old_group = divmod(s - 5, 4)
+            for (m, t) in token:
+                if t == 2:
+                    root(m)
             if is_unit(s):
                 add_bonus(s)
+            if 0 <= old_group[0] < TILES - 1:
+                store(old_group[0], old_group[1], old_group[1] % 2 == 1)
             for (m, t) in token:
                 if t < 2:
                     bn_part(m, 2 * t)
-                if t == 3:
-                    scale_and_shift(m)
                 if t == 0:
                     products(m)
-            if 0 <= done_pair < PAIRS:
+            if has_pair:
                 quantise_w(done_pair, (0, 1))
             if is_unit(s):
                 times_gate(s)
@@ -296,34 +303,45 @@ def tile_full_tmix_params_pc_kernel(tc, y, r, k, v, g_hid, g2, r_k, ln_g, ln_b, 
                 if t < 2:
                     bn_part(m, 2 * t + 1)
                 if t == 1:
-                    variance(m)
-            if 0 <= done_pair < PAIRS:
+                    variance_sums(m)
+            if has_pair:
                 quantise_w(done_pair, (2, 3))
+            for (m, t) in token:
+                if t == 1:
+                    variance(m)
             if is_unit(s):
                 quantise_z(s)
             for (m, t) in token:
                 if t >= 2:
                     dot_sum(m, t - 2)
-            if s == -8:
+                if t == 2:
+                    scale_and_shift(m)
+            if s == -5:
                 turn_ln_and_g_hid()
-            if 0 <= s + 8 < PAIRS:
-                turn_w(s + 8)
-            if is_unit(s + 1):
-                turn_s2(s + 1)
-                gate(s + 1)
+            if 0 <= s + 1 < PAIRS:
+                turn_w(s + 1)
             if is_unit(s + 2):
                 turn_s1(s + 2)
-            if is_unit(s - 1):
-                mx_passes(s - 1)
-            for (m, t) in token:
-                if t == 2:
-                    root(m)
-            if 0 <= s + 8 < PAIRS:
-                regroup_w(s + 8)
+            if is_unit(s + 1):
+                turn_s2(s + 1)
+            if has_group:
+                open_bank(group[0], group[1])
+                for g in range(PASSES):
+                    mx_pass(group[0], g, group[1])
+            if s >= UNITS - PASSES + 1:
+                g = s - (UNITS - PASSES + 1)
+                for n in range(4):
+                    if g == 0:
+                        open_bank(TILES - 1, n)
+                    mx_pass(TILES - 1, g, n)
+            if is_unit(s + 1):
+                gate(s + 1)
+            if 0 <= s + 1 < PAIRS:
+                regroup_w(s + 1)
             if is_unit(s + 2):
                 bonus_heads(s + 2)
                 gain_and_bias(s + 2)
             if is_unit(s + 3):
                 norm_heads(s + 3)
-            if s >= PASSES and s % PASSES == 0:
-                store_tile(s // PASSES - 1)
+        for n in range(4):
+            store(TILES - 1, n, n % 2 == 1)

@@ -24,7 +24,8 @@ HEAD = 64
 HEADS = C // HEAD
 PASSES = 4
 UNITS = TILES * PASSES
-PAIRS = 8
+QUADS = 4
+W_UNITS = QUADS * PASSES
 EPS = 0.00064
 GW = 256
 
@@ -42,6 +43,9 @@ def tile_full_tmix_params_pc_kernel(tc, y, r, k, v, g_hid, g2, r_k, ln_g, ln_b, 
 
         ident = const.tile([P, P], F32, name="ident")
         make_identity(nc, ident[:])
+        warm = const.tile([P, 1], F32, name="warm")
+        nc.vector.memset(warm[:], 1.0)
+        nc.scalar.activation(out=warm[:], in_=warm[:], func=SQRT)
         rk_row = ld.tile([P, C], BF16, name="rk_row", tag="ld")
         nc.vector.memset(rk_row[:].bitcast(U32), 0)
         ln_rows = const.tile([P, 4 * P], BF16, name="ln_rows")
@@ -68,10 +72,10 @@ def tile_full_tmix_params_pc_kernel(tc, y, r, k, v, g_hid, g2, r_k, ln_g, ln_b, 
         def load_v(m):
             v_sb[m] = load(v[m], "v%d" % m)
 
-        def load_w(pair):
-            for b in range(2):
-                row = 256 * pair + P * b
-                w_sb[(pair, b)] = load(W_o[row:row + P, :], "w%d_%d" % (pair, b))
+        def load_w(q):
+            for b in range(4):
+                row = 512 * q + P * b
+                w_sb[(q, b)] = load(W_o[row:row + P, :], "w%d_%d" % (q, b))
 
         load_y(0)
         nc.sync.dma_start(out=rk_row[0:1, :], in_=r_k.rearrange("(o h) i -> o (h i)", o=1))
@@ -79,24 +83,20 @@ def tile_full_tmix_params_pc_kernel(tc, y, r, k, v, g_hid, g2, r_k, ln_g, ln_b, 
         nc.sync.dma_start(out=gh_rows[:].rearrange("t (b d) -> t b d", b=TILES), in_=g_hid.rearrange("b t d -> t b d"))
         nc.sync.dma_start(out=ln_rows[0:4, :], in_=ln_g.rearrange("(a b) -> a b", b=4 * P))
         nc.sync.dma_start(out=ln_rows[4:8, :], in_=ln_b.rearrange("(a b) -> a b", b=4 * P))
+        load_y(1)
         load_v(0)
         for e in range(2):
             nc.sync.dma_start(out=g2_sb[:, e, :], in_=g2.rearrange("(q e) c -> e q c", e=2)[e])
-        load_y(1)
         load_w(0)
-        load_w(1)
         load_rk(1)
-        load_w(2)
-        load_v(1)
-        load_w(3)
         load_y(2)
+        load_w(1)
+        load_v(1)
+        load_w(2)
         load_rk(2)
-        load_w(4)
-        load_w(5)
-        load_w(6)
-        load_v(2)
-        load_w(7)
         load_y(3)
+        load_w(3)
+        load_v(2)
         load_rk(3)
         load_v(3)
 
@@ -104,14 +104,14 @@ def tile_full_tmix_params_pc_kernel(tc, y, r, k, v, g_hid, g2, r_k, ln_g, ln_b, 
         ln_words = const.tile([P, 16], F32, name="ln_words")
         ln_cols = const.tile([P, 32], F32, name="ln_cols")
         gh_t = const.tile([P, 2, 512], BF16, name="gh_t")
-        w_codes = const.tile([P, PASSES, CO], U32, name="w_codes", align_bytes=64)
-        w_scales = const.tile([P, PASSES, CO], U8, name="w_scales", align_bytes=64)
+        w_codes = const.tile([P, QUADS, 4 * 512], U32, name="w_codes", align_bytes=64)
+        w_scales = const.tile([P, QUADS, 4 * 512], U8, name="w_scales", align_bytes=64)
         z_codes = const.tile([P, TILES, 512], U32, name="z_codes", align_bytes=64)
         z_scales = const.tile([P, TILES, 512], U8, name="z_scales", align_bytes=64)
 
         def spread_r_k():
             for j in range(4):
-                acc = psum.tile([P, 512], F32, name="rk_ps%d" % j, tag=("A", "B", "G", "X")[j], bufs=(1, 1, 1, 5)[j])
+                acc = psum.tile([P, 512], F32, name="rk_ps%d" % j, tag=("A", "B", "G", "X")[j], bufs=(1, 1, 2, 4)[j])
                 nc.tensor.matmul(acc[:], lhsT=ones[:], rhs=rk_row[:, 512 * j:512 * j + 512], start=True, stop=True)
                 nc.scalar.copy(out=rk_all[:, 512 * j:512 * j + 512], in_=acc[:])
 
@@ -121,12 +121,12 @@ def tile_full_tmix_params_pc_kernel(tc, y, r, k, v, g_hid, g2, r_k, ln_g, ln_b, 
                 nc.tensor.transpose(ln_ps[:, half, :], ln_rows[:].bitcast(F32)[:, half:2 * P:2], ident[:])
             nc.vector.tensor_copy(out=ln_words[:].rearrange("p (n u) -> p n u", u=2), in_=ln_ps[:, :, 0:8].rearrange("p u n -> p n u"))
             nc.vector.tensor_copy(out=ln_cols[:], in_=ln_words[:].bitcast(BF16))
-            gh_ps = psum.tile([P, 512], F32, name="gh_ps", tag="G", bufs=1)
+            gh_ps = psum.tile([P, 512], F32, name="gh_ps", tag="G", bufs=2)
             for m in range(TILES):
                 nc.tensor.transpose(gh_ps[:, P * m:P * m + P], gh_rows[:].bitcast(F32)[:, P * m:P * m + P], ident[:])
             nc.vector.tensor_copy(out=gh_t[:], in_=gh_ps[:].bitcast(BF16).rearrange("q (n e) -> q e n", e=2))
 
-        bn_out, sums, diff, var_eps, std, a_b, dots, rkw = {}, {}, {}, {}, {}, {}, {}, {}
+        bn_out, sums, minus_mean, var_eps, std, scale, shift, dots, rkw = {}, {}, {}, {}, {}, {}, {}, {}, {}
         s1, s2, s1_ps, s2_ps, gate_ps, e1, z_bf, w_bf, w_ps, out_ps = {}, {}, {}, {}, {}, {}, {}, {}, {}, {}
 
         def bn_part(m, part):
@@ -135,44 +135,49 @@ def tile_full_tmix_params_pc_kernel(tc, y, r, k, v, g_hid, g2, r_k, ln_g, ln_b, 
             for h in range(8 * part, 8 * part + 8):
                 nc.vector.bn_stats(out=bn_out[m][:, h, :], in_=y_sb[m][:, HEAD * h:HEAD * h + HEAD])
 
-        def variance_sums(m):
+        def variance(m):
             st = bn_out[m]
             sums[m] = work.tile([P, HEADS, 2], F32, name="sums%d" % m, tag="sums")
-            nc.vector.tensor_tensor(out=sums[m][:], in0=st[:, :, 1:3], in1=st[:, :, 4:6], op=ADD)
-            diff[m] = work.tile([P, HEADS], F32, name="diff%d" % m, tag="diff")
-            nc.vector.tensor_tensor(out=diff[m][:], in0=st[:, :, 1], in1=st[:, :, 4], op=SUB)
-
-        def variance(m):
+            nc.gpsimd.tensor_tensor(out=sums[m][:], in0=st[:, :, 1:3], in1=st[:, :, 4:6], op=ADD)
+            diff = work.tile([P, HEADS], F32, name="diff%d" % m, tag="diff")
+            nc.gpsimd.tensor_tensor(out=diff[:], in0=st[:, :, 1], in1=st[:, :, 4], op=SUB)
             within = work.tile([P, HEADS], F32, name="within%d" % m, tag="within")
-            nc.vector.tensor_scalar(out=within[:], in0=sums[m][:, :, 1], scalar1=1.0 / HEAD, scalar2=EPS, op0=MUL, op1=ADD)
+            nc.gpsimd.tensor_scalar(out=within[:], in0=sums[m][:, :, 1], scalar1=1.0 / HEAD, scalar2=EPS, op0=MUL, op1=ADD)
             diff2 = work.tile([P, HEADS], F32, name="diffsq%d" % m, tag="diffsq")
-            nc.vector.tensor_tensor(out=diff2[:], in0=diff[m][:], in1=diff[m][:], op=MUL)
+            nc.gpsimd.tensor_tensor(out=diff2[:], in0=diff[:], in1=diff[:], op=MUL)
+            minus_mean[m] = work.tile([P, HEADS], F32, name="mm%d" % m, tag="mm")
+            nc.gpsimd.tensor_scalar(out=minus_mean[m][:], in0=sums[m][:, :, 0], scalar1=-0.5, scalar2=0.0, op0=MUL, op1=ADD)
+            quarter = work.tile([P, HEADS], F32, name="quarter%d" % m, tag="quarter")
+            nc.gpsimd.tensor_scalar(out=quarter[:], in0=diff2[:], scalar1=0.25, scalar2=0.0, op0=MUL, op1=ADD)
             var_eps[m] = work.tile([P, HEADS], F32, name="vareps%d" % m, tag="vareps")
-            nc.vector.scalar_tensor_tensor(out=var_eps[m][:], in0=diff2[:], scalar=0.25, in1=within[:], op0=MUL, op1=ADD)
+            nc.gpsimd.tensor_tensor(out=var_eps[m][:], in0=quarter[:], in1=within[:], op=ADD)
 
         def root(m):
             std[m] = work.tile([P, HEADS], F32, name="std%d" % m, tag="std")
             nc.scalar.activation(out=std[m][:], in_=var_eps[m][:], func=SQRT)
 
         def scale_and_shift(m):
-            a_b[m] = work.tile([P, 2, HEADS], F32, name="ab%d" % m, tag="ab")
-            nc.vector.reciprocal(out=a_b[m][:, 0, :], in_=std[m][:])
-            nc.vector.scalar_tensor_tensor(out=a_b[m][:, 1, :], in0=sums[m][:, :, 0], scalar=-0.5, in1=a_b[m][:, 0, :],
-                                           op0=MUL, op1=MUL)
+            scale[m] = work.tile([P, HEADS], F32, name="scale%d" % m, tag="scale")
+            nc.vector.reciprocal(out=scale[m][:], in_=std[m][:])
+            shift[m] = work.tile([P, HEADS], F32, name="shift%d" % m, tag="shift")
+            nc.gpsimd.tensor_tensor(out=shift[m][:], in0=minus_mean[m][:], in1=scale[m][:], op=MUL)
 
-        def products(m):
-            rkw[m] = work.tile([P, C], F32, name="rkw%d" % m, tag="rkw")
-            dots[m] = work.tile([P, HEADS], F32, name="dot%d" % m, tag="dot")
-            for first in range(0, C, 2 * GW):
-                both = (slice(first, first + GW), slice(first + GW, first + 2 * GW))
-                for cols in both:
-                    nc.gpsimd.tensor_tensor(out=rkw[m][:, cols], in0=r_sb[m][:, cols], in1=k_sb[m][:, cols], op=MUL)
-                for cols in both:
-                    nc.gpsimd.tensor_tensor(out=rkw[m][:, cols], in0=rkw[m][:, cols], in1=rk_all[:, cols], op=MUL)
+        def product(u):
+            m, g = divmod(u, PASSES)
+            rkw[u] = work.tile([P, 512], F32, name="rkw%d" % u, tag="rkw", bufs=4)
+            if g == 0:
+                dots[m] = work.tile([P, HEADS], F32, name="dot%d" % m, tag="dot")
+            both = [slice(first, first + GW) for first in range(0, 512, GW)]
+            rows = (r_sb[m][:, 512 * g:512 * g + 512], k_sb[m][:, 512 * g:512 * g + 512], rk_all[:, 512 * g:512 * g + 512])
+            for cols in both:
+                nc.gpsimd.tensor_tensor(out=rkw[u][:, cols], in0=rows[0][:, cols], in1=rows[1][:, cols], op=MUL)
+            for cols in both:
+                nc.gpsimd.tensor_tensor(out=rkw[u][:, cols], in0=rkw[u][:, cols], in1=rows[2][:, cols], op=MUL)
 
-        def dot_sum(m, g):
+        def dot_sum(u):
+            m, g = divmod(u, PASSES)
             nc.vector.tensor_reduce(out=dots[m][:, 8 * g:8 * g + 8],
-                                    in_=rkw[m][:, 512 * g:512 * g + 512].rearrange("t (h i) -> t h i", i=HEAD),
+                                    in_=rkw[u][:].rearrange("t (h i) -> t h i", i=HEAD),
                                     axis=AXIS_X, op=ADD)
 
         def split_view(tile_ap, h):
@@ -185,7 +190,7 @@ def tile_full_tmix_params_pc_kernel(tc, y, r, k, v, g_hid, g2, r_k, ln_g, ln_b, 
                 h = 8 * g + i
                 nc.scalar.activation(out=s1[u][:, :, 16 * i:16 * i + 16],
                                      in_=split_view(y_sb[m], h), func=IDENTITY,
-                                     bias=a_b[m][:, 1, h:h + 1], scale=a_b[m][:, 0, h:h + 1])
+                                     bias=shift[m][:, h:h + 1], scale=scale[m][:, h:h + 1])
 
         def bonus_heads(u):
             m, g = divmod(u, PASSES)
@@ -207,7 +212,7 @@ def tile_full_tmix_params_pc_kernel(tc, y, r, k, v, g_hid, g2, r_k, ln_g, ln_b, 
 
         def gate(u):
             m, g = divmod(u, PASSES)
-            gate_ps[u] = psum.tile([P, 4, P], F32, name="gps%d" % u, tag="G", bufs=1)
+            gate_ps[u] = psum.tile([P, 4, P], F32, name="gps%d" % u, tag="G", bufs=2)
             for t in range(4):
                 for e in range(2):
                     every_fourth = g2_sb[:, e, 512 * g:512 * g + 512].rearrange("q (p f) -> q f p", f=4)[:, t, :]
@@ -226,46 +231,53 @@ def tile_full_tmix_params_pc_kernel(tc, y, r, k, v, g_hid, g2, r_k, ln_g, ln_b, 
             nc.vector.tensor_tensor(out=e1[u][:], in0=e1[u][:], in1=s2_ps[u][:], op=ADD)
 
         def times_gate(u):
-            z_bf[u] = work.tile([P, P, 4], BF16, name="z%d" % u, tag="z", bufs=3, align_bytes=64)
-            nc.vector.tensor_tensor(out=z_bf[u][:], in0=e1[u][:].rearrange("p t r -> p r t"),
+            m, g = divmod(u, PASSES)
+            if g == 0:
+                z_bf[m] = work.tile([P, 512, 4], BF16, name="z%d" % m, tag="z", bufs=2, align_bytes=64)
+            nc.vector.tensor_tensor(out=z_bf[m][:, P * g:P * g + P, :], in0=e1[u][:].rearrange("p t r -> p r t"),
                                     in1=gate_ps[u][:].rearrange("p t r -> p r t"), op=MUL)
 
-        def quantise_z(u):
-            m, g = divmod(u, PASSES)
-            nc.vector.quantize_mx(out=z_codes[:, m, P * g:P * g + P].bitcast(FP8X4), scales=z_scales[:, m, P * g:P * g + P],
-                                  in_=z_bf[u][:].rearrange("p r t -> p (r t)"))
+        def quantise_z(m, first, last):
+            cols = slice(P * first, P * last + P)
+            nc.vector.quantize_mx(out=z_codes[:, m, cols].bitcast(FP8X4), scales=z_scales[:, m, cols],
+                                  in_=z_bf[m][:, cols, :].rearrange("p r t -> p (r t)"))
 
-        def turn_w(pair):
-            for g in range(PASSES):
-                w_ps[(pair, g)] = psum.tile([P, 2, 256], F32, name="wps%d_%d" % (pair, g), tag="X", bufs=5)
+        def turn_w(w):
+            q, g = divmod(w, PASSES)
+            for pair in range(2):
+                w_ps[(w, pair)] = psum.tile([P, 2, 256], F32, name="wps%d_%d" % (w, pair), tag="X", bufs=4)
                 for half in range(2):
                     for b in range(2):
-                        nc.tensor.transpose(w_ps[(pair, g)][:, half, P * b:P * b + P],
-                                            w_sb[(pair, b)][:].bitcast(F32)[:, 256 * g + half:256 * g + 256:2], ident[:])
+                        nc.tensor.transpose(w_ps[(w, pair)][:, half, P * b:P * b + P],
+                                            w_sb[(q, 2 * pair + b)][:].bitcast(F32)[:, 256 * g + half:256 * g + 256:2], ident[:])
 
-        def regroup_w(pair):
-            w_bf[pair] = work.tile([P, 4096], BF16, name="wbf%d" % pair, tag="wbf", bufs=2, align_bytes=64)
-            words = w_bf[pair][:].bitcast(F32).rearrange("p (g c u) -> p g c u", g=PASSES, u=2)
-            for g in range(PASSES):
-                nc.scalar.copy(out=words[:, g, :, :], in_=w_ps[(pair, g)][:].rearrange("p u c -> p c u"))
+        def regroup_w(w):
+            if w % 2 == 0:
+                w_bf[w // 2] = work.tile([P, 4096], BF16, name="wbf%d" % w, tag="wbf", bufs=2, align_bytes=64)
+            words = w_bf[w // 2][:].bitcast(F32).rearrange("p (c u) -> p c u", u=2)
+            for pair in range(2):
+                first = 512 * (w % 2) + 256 * pair
+                if w % 4 == 1 and pair == 1:
+                    nc.vector.tensor_copy(out=words[:, first:first + 256, :], in_=w_ps[(w, pair)][:].rearrange("p u c -> p c u"))
+                else:
+                    nc.scalar.copy(out=words[:, first:first + 256, :], in_=w_ps[(w, pair)][:].rearrange("p u c -> p c u"))
 
-        def quantise_w(pair, passes):
-            for g in passes:
-                nc.vector.quantize_mx(out=w_codes[:, g, 256 * pair:256 * pair + 256].bitcast(FP8X4),
-                                      scales=w_scales[:, g, 256 * pair:256 * pair + 256],
-                                      in_=w_bf[pair][:, 1024 * g:1024 * g + 1024])
+        def quantise_w(two):
+            q, half = divmod(two, 2)
+            nc.vector.quantize_mx(out=w_codes[:, q, 1024 * half:1024 * half + 1024].bitcast(FP8X4),
+                                  scales=w_scales[:, q, 1024 * half:1024 * half + 1024], in_=w_bf[two][:])
 
         def mx_pass(m, g, n):
             nc.tensor.matmul_mx(out=out_ps[(m, n)][:],
                                 lhsT=z_codes[:, m, P * g:P * g + P].bitcast(FP8X4), lhsT_scale=z_scales[:, m, P * g:P * g + P],
-                                rhs=w_codes[:, g, 512 * n:512 * n + 512].bitcast(FP8X4), rhs_scale=w_scales[:, g, 512 * n:512 * n + 512],
+                                rhs=w_codes[:, n, 512 * g:512 * g + 512].bitcast(FP8X4), rhs_scale=w_scales[:, n, 512 * g:512 * g + 512],
                                 start=(g == 0), stop=(g == PASSES - 1))
 
         def open_bank(m, n):
-            out_ps[(m, n)] = psum.tile([P, 512], F32, name="ops%d_%d" % (m, n), tag="X", bufs=5)
+            out_ps[(m, n)] = psum.tile([P, 512], F32, name="ops%d_%d" % (m, n), tag="X", bufs=4)
 
         def store(m, n, on_vector):
-            res = work.tile([P, 512], F32, name="res%d_%d" % (m, n), tag="res", bufs=4)
+            res = work.tile([P, 512], F32, name="res%d_%d" % (m, n), tag="res", bufs=6)
             if on_vector:
                 nc.vector.tensor_copy(out=res[:], in_=out_ps[(m, n)][:])
             else:
@@ -275,73 +287,83 @@ def tile_full_tmix_params_pc_kernel(tc, y, r, k, v, g_hid, g2, r_k, ln_g, ln_b, 
         def is_unit(u):
             return 0 <= u < UNITS
 
+        def is_w_unit(w):
+            return 0 <= w < W_UNITS
+
+        def groups_of_step(s):
+            if 5 <= s < 9:
+                return [(0, s - 5)]
+            if 9 <= s < 11:
+                return [(1, 2 * (s - 9)), (1, 2 * (s - 9) + 1)]
+            if 12 <= s < 14:
+                return [(2, 2 * (s - 12)), (2, 2 * (s - 12) + 1)]
+            return []
+
         spread_r_k()
-        for s in range(-6, UNITS + 1):
-            token = [(m, s - (4 * m - 6)) for m in range(TILES) if 0 <= s - (4 * m - 6) < 6]
-            done_pair = s
-            has_pair = 0 <= done_pair < PAIRS
-            group = divmod(s - 4, 4)
-            has_group = 0 <= group[0] < TILES - 1
-            old_group = divmod(s - 5, 4)
-            for (m, t) in token:
-                if t == 2:
-                    root(m)
+        for s in range(-7, UNITS + 1):
             if is_unit(s):
                 add_bonus(s)
-            if 0 <= old_group[0] < TILES - 1:
-                store(old_group[0], old_group[1], old_group[1] % 2 == 1)
-            for (m, t) in token:
-                if t < 2:
-                    bn_part(m, 2 * t)
-                if t == 0:
-                    products(m)
-            if has_pair:
-                quantise_w(done_pair, (0, 1))
+            for m in range(TILES):
+                if s == 4 * m - 2:
+                    scale_and_shift(m)
+            if is_w_unit(2 * (s - 1)):
+                quantise_w(s - 1)
             if is_unit(s):
                 times_gate(s)
-            for (m, t) in token:
-                if t < 2:
-                    bn_part(m, 2 * t + 1)
-                if t == 1:
-                    variance_sums(m)
-            if has_pair:
-                quantise_w(done_pair, (2, 3))
-            for (m, t) in token:
-                if t == 1:
+            for m in range(TILES):
+                part = s - (4 * m - 7)
+                if 0 <= part < 4:
+                    bn_part(m, part)
+            if s == -4:
+                variance(0)
+            if is_unit(s + 4):
+                product(s + 4)
+            for m in range(1, TILES):
+                if s == 4 * m - 4:
                     variance(m)
+            for (m, n) in groups_of_step(s - 1):
+                if n % 2 == 1:
+                    store(m, n, True)
+            if is_unit(s + 3):
+                dot_sum(s + 3)
             if is_unit(s):
-                quantise_z(s)
-            for (m, t) in token:
-                if t >= 2:
-                    dot_sum(m, t - 2)
-                if t == 2:
-                    scale_and_shift(m)
-            if s == -5:
+                m, g = divmod(s, PASSES)
+                if m == TILES - 1:
+                    quantise_z(m, g, g)
+                elif g == PASSES - 1:
+                    quantise_z(m, 0, g)
+            if s == -3:
                 turn_ln_and_g_hid()
-            if 0 <= s + 1 < PAIRS:
-                turn_w(s + 1)
-            if is_unit(s + 2):
-                turn_s1(s + 2)
+            for w in (2 * s, 2 * s + 1):
+                if is_w_unit(w):
+                    turn_w(w)
             if is_unit(s + 1):
+                turn_s1(s + 1)
                 turn_s2(s + 1)
-            if has_group:
-                open_bank(group[0], group[1])
+                gate(s + 1)
+            for (m, n) in groups_of_step(s):
+                open_bank(m, n)
                 for g in range(PASSES):
-                    mx_pass(group[0], g, group[1])
-            if s >= UNITS - PASSES + 1:
-                g = s - (UNITS - PASSES + 1)
+                    mx_pass(m, g, n)
+            for g in {14: (0, 1), 15: (2,), 16: (3,)}.get(s, ()):
                 for n in range(4):
                     if g == 0:
                         open_bank(TILES - 1, n)
                     mx_pass(TILES - 1, g, n)
-            if is_unit(s + 1):
-                gate(s + 1)
-            if 0 <= s + 1 < PAIRS:
-                regroup_w(s + 1)
+            for w in (2 * s, 2 * s + 1):
+                if is_w_unit(w):
+                    regroup_w(w)
             if is_unit(s + 2):
                 bonus_heads(s + 2)
-                gain_and_bias(s + 2)
-            if is_unit(s + 3):
-                norm_heads(s + 3)
+            for (m, n) in groups_of_step(s - 1):
+                if n % 2 == 0:
+                    store(m, n, False)
+            if is_unit(s + 1):
+                gain_and_bias(s + 1)
+            for m in range(TILES):
+                if s == 4 * m - 3:
+                    root(m)
+            if is_unit(s + 2):
+                norm_heads(s + 2)
         for n in range(4):
             store(TILES - 1, n, n % 2 == 1)

@@ -9,7 +9,6 @@ U32 = mybir.dt.uint32
 U8 = mybir.dt.uint8
 FP8X4 = mybir.dt.float8_e4m3fn_x4
 ADD = mybir.AluOpType.add
-SUB = mybir.AluOpType.subtract
 MUL = mybir.AluOpType.mult
 IDENTITY = mybir.ActivationFunctionType.Identity
 COPY = mybir.ActivationFunctionType.Copy
@@ -36,7 +35,7 @@ def tile_full_tmix_params_pc_kernel(tc, y, r, k, v, g_hid, g2, r_k, ln_g, ln_b, 
     nc = tc.nc
     with ExitStack() as ctx:
         const = ctx.enter_context(tc.tile_pool(name="const", bufs=1))
-        ld = ctx.enter_context(tc.tile_pool(name="ld", bufs=26))
+        ld = ctx.enter_context(tc.tile_pool(name="ld", bufs=25))
         work = ctx.enter_context(tc.tile_pool(name="work", bufs=2))
         psum = ctx.enter_context(tc.psum_pool(name="psum", bufs=1))
         ctx.enter_context(tc.manual_schedule())
@@ -126,58 +125,40 @@ def tile_full_tmix_params_pc_kernel(tc, y, r, k, v, g_hid, g2, r_k, ln_g, ln_b, 
                 nc.tensor.transpose(gh_ps[:, P * m:P * m + P], gh_rows[:].bitcast(F32)[:, P * m:P * m + P], ident[:])
             nc.vector.tensor_copy(out=gh_t[:], in_=gh_ps[:].bitcast(BF16).rearrange("q (n e) -> q e n", e=2))
 
-        bn_out, sums, minus_mean, var_eps, std, scale, shift, dots, rkw = {}, {}, {}, {}, {}, {}, {}, {}, {}
+        bn_out, std, a_b, dots, rkw = {}, {}, {}, {}, {}
         s1, s2, s1_ps, s2_ps, gate_ps, e1, z_bf, w_bf, w_ps, out_ps = {}, {}, {}, {}, {}, {}, {}, {}, {}, {}
 
         def bn_part(m, part):
             if part == 0:
-                bn_out[m] = work.tile([P, HEADS, 6], F32, name="bn%d" % m, tag="bn")
-            for h in range(8 * part, 8 * part + 8):
-                nc.vector.bn_stats(out=bn_out[m][:, h, :], in_=y_sb[m][:, HEAD * h:HEAD * h + HEAD])
-
-        def variance(m):
-            st = bn_out[m]
-            sums[m] = work.tile([P, HEADS, 2], F32, name="sums%d" % m, tag="sums")
-            nc.gpsimd.tensor_tensor(out=sums[m][:], in0=st[:, :, 1:3], in1=st[:, :, 4:6], op=ADD)
-            diff = work.tile([P, HEADS], F32, name="diff%d" % m, tag="diff")
-            nc.gpsimd.tensor_tensor(out=diff[:], in0=st[:, :, 1], in1=st[:, :, 4], op=SUB)
-            within = work.tile([P, HEADS], F32, name="within%d" % m, tag="within")
-            nc.gpsimd.tensor_scalar(out=within[:], in0=sums[m][:, :, 1], scalar1=1.0 / HEAD, scalar2=EPS, op0=MUL, op1=ADD)
-            diff2 = work.tile([P, HEADS], F32, name="diffsq%d" % m, tag="diffsq")
-            nc.gpsimd.tensor_tensor(out=diff2[:], in0=diff[:], in1=diff[:], op=MUL)
-            minus_mean[m] = work.tile([P, HEADS], F32, name="mm%d" % m, tag="mm")
-            nc.gpsimd.tensor_scalar(out=minus_mean[m][:], in0=sums[m][:, :, 0], scalar1=-0.5, scalar2=0.0, op0=MUL, op1=ADD)
-            quarter = work.tile([P, HEADS], F32, name="quarter%d" % m, tag="quarter")
-            nc.gpsimd.tensor_scalar(out=quarter[:], in0=diff2[:], scalar1=0.25, scalar2=0.0, op0=MUL, op1=ADD)
-            var_eps[m] = work.tile([P, HEADS], F32, name="vareps%d" % m, tag="vareps")
-            nc.gpsimd.tensor_tensor(out=var_eps[m][:], in0=quarter[:], in1=within[:], op=ADD)
+                bn_out[m] = work.tile([P, HEADS, 3], F32, name="bn%d" % m, tag="bn")
+            for pair in range(4 * part, 4 * part + 4):
+                two_heads = y_sb[m][:, 2 * HEAD * pair:2 * HEAD * pair + 2 * HEAD].rearrange("t (h i) -> t i h", h=2)
+                nc.vector.bn_stats(out=bn_out[m][:, 2 * pair:2 * pair + 2, :].rearrange("t h s -> t (h s)"), in_=two_heads)
 
         def root(m):
             std[m] = work.tile([P, HEADS], F32, name="std%d" % m, tag="std")
-            nc.scalar.activation(out=std[m][:], in_=var_eps[m][:], func=SQRT)
+            nc.scalar.activation(out=std[m][:], in_=bn_out[m][:, :, 2], func=SQRT, scale=1.0 / HEAD, bias=EPS)
 
         def scale_and_shift(m):
-            scale[m] = work.tile([P, HEADS], F32, name="scale%d" % m, tag="scale")
-            nc.vector.reciprocal(out=scale[m][:], in_=std[m][:])
-            shift[m] = work.tile([P, HEADS], F32, name="shift%d" % m, tag="shift")
-            nc.gpsimd.tensor_tensor(out=shift[m][:], in0=minus_mean[m][:], in1=scale[m][:], op=MUL)
+            a_b[m] = work.tile([P, 2, HEADS], F32, name="ab%d" % m, tag="ab")
+            nc.vector.reciprocal(out=a_b[m][:, 0, :], in_=std[m][:])
+            nc.vector.scalar_tensor_tensor(out=a_b[m][:, 1, :], in0=bn_out[m][:, :, 1], scalar=-1.0, in1=a_b[m][:, 0, :],
+                                           op0=MUL, op1=MUL)
 
-        def product(u):
-            m, g = divmod(u, PASSES)
-            rkw[u] = work.tile([P, 512], F32, name="rkw%d" % u, tag="rkw", bufs=4)
-            if g == 0:
-                dots[m] = work.tile([P, HEADS], F32, name="dot%d" % m, tag="dot")
-            both = [slice(first, first + GW) for first in range(0, 512, GW)]
-            rows = (r_sb[m][:, 512 * g:512 * g + 512], k_sb[m][:, 512 * g:512 * g + 512], rk_all[:, 512 * g:512 * g + 512])
-            for cols in both:
-                nc.gpsimd.tensor_tensor(out=rkw[u][:, cols], in0=rows[0][:, cols], in1=rows[1][:, cols], op=MUL)
-            for cols in both:
-                nc.gpsimd.tensor_tensor(out=rkw[u][:, cols], in0=rkw[u][:, cols], in1=rows[2][:, cols], op=MUL)
+        def products(m):
+            rkw[m] = work.tile([P, C], F32, name="rkw%d" % m, tag="rkw")
+            dots[m] = work.tile([P, HEADS], F32, name="dot%d" % m, tag="dot")
+            for first in range(0, C, 2 * GW):
+                both = (slice(first, first + GW), slice(first + GW, first + 2 * GW))
+                for cols in both:
+                    nc.gpsimd.tensor_tensor(out=rkw[m][:, cols], in0=r_sb[m][:, cols], in1=k_sb[m][:, cols], op=MUL)
+                for cols in both:
+                    nc.gpsimd.tensor_tensor(out=rkw[m][:, cols], in0=rkw[m][:, cols], in1=rk_all[:, cols], op=MUL)
 
         def dot_sum(u):
             m, g = divmod(u, PASSES)
             nc.vector.tensor_reduce(out=dots[m][:, 8 * g:8 * g + 8],
-                                    in_=rkw[u][:].rearrange("t (h i) -> t h i", i=HEAD),
+                                    in_=rkw[m][:, 512 * g:512 * g + 512].rearrange("t (h i) -> t h i", i=HEAD),
                                     axis=AXIS_X, op=ADD)
 
         def split_view(tile_ap, h):
@@ -190,7 +171,7 @@ def tile_full_tmix_params_pc_kernel(tc, y, r, k, v, g_hid, g2, r_k, ln_g, ln_b, 
                 h = 8 * g + i
                 nc.scalar.activation(out=s1[u][:, :, 16 * i:16 * i + 16],
                                      in_=split_view(y_sb[m], h), func=IDENTITY,
-                                     bias=shift[m][:, h:h + 1], scale=scale[m][:, h:h + 1])
+                                     bias=a_b[m][:, 1, h:h + 1], scale=a_b[m][:, 0, h:h + 1])
 
         def bonus_heads(u):
             m, g = divmod(u, PASSES)
@@ -277,7 +258,7 @@ def tile_full_tmix_params_pc_kernel(tc, y, r, k, v, g_hid, g2, r_k, ln_g, ln_b, 
             out_ps[(m, n)] = psum.tile([P, 512], F32, name="ops%d_%d" % (m, n), tag="X", bufs=4)
 
         def store(m, n, on_vector):
-            res = work.tile([P, 512], F32, name="res%d_%d" % (m, n), tag="res", bufs=6)
+            res = work.tile([P, 512], F32, name="res%d_%d" % (m, n), tag="res", bufs=4)
             if on_vector:
                 nc.vector.tensor_copy(out=res[:], in_=out_ps[(m, n)][:])
             else:
@@ -314,13 +295,8 @@ def tile_full_tmix_params_pc_kernel(tc, y, r, k, v, g_hid, g2, r_k, ln_g, ln_b, 
                 part = s - (4 * m - 7)
                 if 0 <= part < 4:
                     bn_part(m, part)
-            if s == -4:
-                variance(0)
-            if is_unit(s + 4):
-                product(s + 4)
-            for m in range(1, TILES):
-                if s == 4 * m - 4:
-                    variance(m)
+                if s == 4 * m - 6:
+                    products(m)
             for (m, n) in groups_of_step(s - 1):
                 if n % 2 == 1:
                     store(m, n, True)

@@ -281,20 +281,20 @@ def tile_full_tmix_params_pc_kernel(tc, y, r, k, v, g_hid, g2, r_k, ln_g, ln_b, 
             return []
 
         spread_r_k()
-        for s in range(-7, UNITS + 1):
+        for s in range(-6, UNITS + 1):
+            for m in range(TILES):
+                if s == 4 * m - 4:
+                    root(m)
             if is_unit(s):
                 add_bonus(s)
-            for m in range(TILES):
-                if s == 4 * m - 2:
-                    scale_and_shift(m)
             if is_w_unit(2 * (s - 1)):
                 quantise_w(s - 1)
             if is_unit(s):
                 times_gate(s)
             for m in range(TILES):
-                part = s - (4 * m - 7)
-                if 0 <= part < 4:
-                    bn_part(m, part)
+                if s in (4 * m - 6, 4 * m - 5):
+                    bn_part(m, 2 * (s - 4 * m + 6))
+                    bn_part(m, 2 * (s - 4 * m + 6) + 1)
                 if s == 4 * m - 6:
                     products(m)
             for (m, n) in groups_of_step(s - 1):
@@ -302,19 +302,23 @@ def tile_full_tmix_params_pc_kernel(tc, y, r, k, v, g_hid, g2, r_k, ln_g, ln_b, 
                     store(m, n, True)
             if is_unit(s + 3):
                 dot_sum(s + 3)
+            for m in range(TILES):
+                if s == 4 * m - 4:
+                    scale_and_shift(m)
             if is_unit(s):
                 m, g = divmod(s, PASSES)
                 if m == TILES - 1:
                     quantise_z(m, g, g)
                 elif g == PASSES - 1:
                     quantise_z(m, 0, g)
-            if s == -3:
+            if s == -4:
                 turn_ln_and_g_hid()
             for w in (2 * s, 2 * s + 1):
                 if is_w_unit(w):
                     turn_w(w)
+            if is_unit(s + 2):
+                turn_s1(s + 2)
             if is_unit(s + 1):
-                turn_s1(s + 1)
                 turn_s2(s + 1)
                 gate(s + 1)
             for (m, n) in groups_of_step(s):
@@ -334,12 +338,9 @@ def tile_full_tmix_params_pc_kernel(tc, y, r, k, v, g_hid, g2, r_k, ln_g, ln_b, 
             for (m, n) in groups_of_step(s - 1):
                 if n % 2 == 0:
                     store(m, n, False)
-            if is_unit(s + 1):
-                gain_and_bias(s + 1)
-            for m in range(TILES):
-                if s == 4 * m - 3:
-                    root(m)
             if is_unit(s + 2):
-                norm_heads(s + 2)
+                gain_and_bias(s + 2)
+            if is_unit(s + 3):
+                norm_heads(s + 3)
         for n in range(4):
             store(TILES - 1, n, n % 2 == 1)

@@ -191,10 +191,11 @@ def tile_full_tmix_params_pc_kernel(tc, y, r, k, v, g_hid, g2, r_k, ln_g, ln_b, 
             for t in range(4):
                 nc.tensor.transpose(s2_ps[u][:, t, :], s2[u][:, t, :], ident[:])
 
-        def gate(u):
+        def gate(u, slots):
             m, g = divmod(u, PASSES)
-            gate_ps[u] = psum.tile([P, 4, P], F32, name="gps%d" % u, tag="G", bufs=2)
-            for t in range(4):
+            if slots[0] == 0:
+                gate_ps[u] = psum.tile([P, 4, P], F32, name="gps%d" % u, tag="G", bufs=2)
+            for t in slots:
                 for e in range(2):
                     every_fourth = g2_sb[:, e, 512 * g:512 * g + 512].rearrange("q (p f) -> q f p", f=4)[:, t, :]
                     nc.tensor.matmul(gate_ps[u][:, t, :], lhsT=every_fourth, rhs=gh_t[:, e, P * m:P * m + P],
@@ -227,6 +228,8 @@ def tile_full_tmix_params_pc_kernel(tc, y, r, k, v, g_hid, g2, r_k, ln_g, ln_b, 
             q, g = divmod(w, PASSES)
             for pair in range(2):
                 w_ps[(w, pair)] = psum.tile([P, 2, 256], F32, name="wps%d_%d" % (w, pair), tag="X", bufs=4)
+                if pair == 0:
+                    nc.tensor.matmul(w_ps[(w, pair)][:, 0, 0:P], lhsT=ident[:], rhs=ident[:], start=True, stop=True)
                 for half in range(2):
                     for b in range(2):
                         nc.tensor.transpose(w_ps[(w, pair)][:, half, P * b:P * b + P],
@@ -313,14 +316,15 @@ def tile_full_tmix_params_pc_kernel(tc, y, r, k, v, g_hid, g2, r_k, ln_g, ln_b, 
                     quantise_z(m, 0, g)
             if s == -4:
                 turn_ln_and_g_hid()
-            for w in (2 * s, 2 * s + 1):
-                if is_w_unit(w):
-                    turn_w(w)
+            for half in range(2):
+                if is_w_unit(2 * s + half):
+                    turn_w(2 * s + half)
+                if is_unit(s + 1):
+                    gate(s + 1, (2 * half, 2 * half + 1))
             if is_unit(s + 2):
                 turn_s1(s + 2)
             if is_unit(s + 1):
                 turn_s2(s + 1)
-                gate(s + 1)
             for (m, n) in groups_of_step(s):
                 open_bank(m, n)
                 for g in range(PASSES):

@@ -228,7 +228,9 @@ def tile_full_tmix_params_pc_kernel(tc, y, r, k, v, g_hid, g2, r_k, ln_g, ln_b, 
             q, g = divmod(w, PASSES)
             for pair in range(2):
                 w_ps[(w, pair)] = psum.tile([P, 2, 256], F32, name="wps%d_%d" % (w, pair), tag="X", bufs=4)
-                if pair == 0:
+                if w < 4:
+                    nc.tensor.matmul(w_ps[(w, pair)][:].rearrange("p u c -> p (u c)"), lhsT=ones[:], rhs=rk_all[:, 0:512], start=True, stop=True)
+                elif pair == 0 or w < 10:
                     nc.tensor.matmul(w_ps[(w, pair)][:, 0, 0:P], lhsT=ident[:], rhs=ident[:], start=True, stop=True)
                 for half in range(2):
                     for b in range(2):

@@ -228,9 +228,9 @@ def tile_full_tmix_params_pc_kernel(tc, y, r, k, v, g_hid, g2, r_k, ln_g, ln_b, 
             q, g = divmod(w, PASSES)
             for pair in range(2):
                 w_ps[(w, pair)] = psum.tile([P, 2, 256], F32, name="wps%d_%d" % (w, pair), tag="X", bufs=4)
-                if w < 4:
+                for dummy in range(5 if w == 0 and pair == 0 else 0):
                     nc.tensor.matmul(w_ps[(w, pair)][:].rearrange("p u c -> p (u c)"), lhsT=ones[:], rhs=rk_all[:, 0:512], start=True, stop=True)
-                elif pair == 0 or w < 10:
+                if pair == 0 or w < 12:
                     nc.tensor.matmul(w_ps[(w, pair)][:, 0, 0:P], lhsT=ident[:], rhs=ident[:], start=True, stop=True)
                 for half in range(2):
                     for b in range(2):
@@ -279,8 +279,8 @@ def tile_full_tmix_params_pc_kernel(tc, y, r, k, v, g_hid, g2, r_k, ln_g, ln_b, 
         def groups_of_step(s):
             if 5 <= s < 9:
                 return [(0, s - 5)]
-            if 9 <= s < 11:
-                return [(1, 2 * (s - 9)), (1, 2 * (s - 9) + 1)]
+            if 9 <= s < 12:
+                return [(1, 0)] if s == 9 else [(1, 1), (1, 2)] if s == 10 else [(1, 3)]
             if 12 <= s < 14:
                 return [(2, 2 * (s - 12)), (2, 2 * (s - 12) + 1)]
             return []
@@ -339,6 +339,8 @@ def tile_full_tmix_params_pc_kernel(tc, y, r, k, v, g_hid, g2, r_k, ln_g, ln_b, 
             for w in (2 * s, 2 * s + 1):
                 if is_w_unit(w):
                     regroup_w(w)
+            if is_unit(s + 3):
+                norm_heads(s + 3)
             if is_unit(s + 2):
                 bonus_heads(s + 2)
             for (m, n) in groups_of_step(s - 1):
@@ -346,7 +348,5 @@ def tile_full_tmix_params_pc_kernel(tc, y, r, k, v, g_hid, g2, r_k, ln_g, ln_b, 
                     store(m, n, False)
             if is_unit(s + 2):
                 gain_and_bias(s + 2)
-            if is_unit(s + 3):
-                norm_heads(s + 3)
         for n in range(4):
             store(TILES - 1, n, n % 2 == 1)

from contextlib import ExitStack

import concourse.mybir as mybir
from concourse.masks import make_identity

F32 = mybir.dt.float32
BF16 = mybir.dt.bfloat16
U32 = mybir.dt.uint32
U8 = mybir.dt.uint8
FP8X4 = mybir.dt.float8_e4m3fn_x4
ADD = mybir.AluOpType.add
MUL = mybir.AluOpType.mult
IDENTITY = mybir.ActivationFunctionType.Identity
COPY = mybir.ActivationFunctionType.Copy
SQRT = mybir.ActivationFunctionType.Sqrt
AXIS_X = mybir.AxisListType.X

P = 128
TILES = 4
C = 2048
CO = 2048
HEAD = 64
HEADS = C // HEAD
PASSES = 4
UNITS = TILES * PASSES
QUADS = 4
W_UNITS = QUADS * PASSES
EPS = 0.00064
GW = 256

FLOPS = 2 * 512 * 2048 * 2048 + 2 * 512 * 256 * 2048


def tile_full_tmix_params_pc_kernel(tc, y, r, k, v, g_hid, g2, r_k, ln_g, ln_b, W_o, out):
    nc = tc.nc
    with ExitStack() as ctx:
        const = ctx.enter_context(tc.tile_pool(name="const", bufs=1))
        ld = ctx.enter_context(tc.tile_pool(name="ld", bufs=25))
        work = ctx.enter_context(tc.tile_pool(name="work", bufs=2))
        psum = ctx.enter_context(tc.psum_pool(name="psum", bufs=1))
        ctx.enter_context(tc.manual_schedule())

        ident = const.tile([P, P], F32, name="ident")
        make_identity(nc, ident[:])
        warm = const.tile([P, 1], F32, name="warm")
        nc.vector.memset(warm[:], 1.0)
        nc.scalar.activation(out=warm[:], in_=warm[:], func=SQRT)
        rk_row = ld.tile([P, C], BF16, name="rk_row", tag="ld")
        nc.vector.memset(rk_row[:].bitcast(U32), 0)
        ln_rows = const.tile([P, 4 * P], BF16, name="ln_rows")
        nc.vector.memset(ln_rows[:].bitcast(U32), 0)
        ones = const.tile([P, P], BF16, name="ones")
        nc.vector.memset(ones[:], 1.0)
        gh_rows = const.tile([P, TILES * 256], BF16, name="gh_rows")
        g2_sb = const.tile([P, 2, C], BF16, name="g2_sb")

        y_sb, r_sb, k_sb, v_sb, w_sb = {}, {}, {}, {}, {}

        def load(src, label):
            t = ld.tile([P, C], BF16, name=label, tag="ld")
            nc.sync.dma_start(out=t[:], in_=src)
            return t

        def load_y(m):
            y_sb[m] = load(y[m], "y%d" % m)

        def load_rk(m):
            r_sb[m] = load(r[m], "r%d" % m)
            k_sb[m] = load(k[m], "k%d" % m)

        def load_v(m):
            v_sb[m] = load(v[m], "v%d" % m)

        def load_w(q):
            for b in range(4):
                row = 512 * q + P * b
                w_sb[(q, b)] = load(W_o[row:row + P, :], "w%d_%d" % (q, b))

        load_y(0)
        nc.sync.dma_start(out=rk_row[0:1, :], in_=r_k.rearrange("(o h) i -> o (h i)", o=1))
        load_rk(0)
        nc.sync.dma_start(out=gh_rows[:].rearrange("t (b d) -> t b d", b=TILES), in_=g_hid.rearrange("b t d -> t b d"))
        nc.sync.dma_start(out=ln_rows[0:4, :], in_=ln_g.rearrange("(a b) -> a b", b=4 * P))
        nc.sync.dma_start(out=ln_rows[4:8, :], in_=ln_b.rearrange("(a b) -> a b", b=4 * P))
        load_y(1)
        load_v(0)
        for e in range(2):
            nc.sync.dma_start(out=g2_sb[:, e, :], in_=g2.rearrange("(q e) c -> e q c", e=2)[e])
        load_w(0)
        load_rk(1)
        load_y(2)
        load_w(1)
        load_v(1)
        load_w(2)
        load_rk(2)
        load_y(3)
        load_w(3)
        load_v(2)
        load_rk(3)
        load_v(3)

        rk_all = const.tile([P, C], BF16, name="rk_all")
        ln_words = const.tile([P, 16], F32, name="ln_words")
        ln_cols = const.tile([P, 32], F32, name="ln_cols")
        gh_t = const.tile([P, 2, 512], BF16, name="gh_t")
        w_codes = const.tile([P, QUADS, 4 * 512], U32, name="w_codes", align_bytes=64)
        w_scales = const.tile([P, QUADS, 4 * 512], U8, name="w_scales", align_bytes=64)
        z_codes = const.tile([P, TILES, 512], U32, name="z_codes", align_bytes=64)
        z_scales = const.tile([P, TILES, 512], U8, name="z_scales", align_bytes=64)

        def spread_r_k():
            for j in range(4):
                acc = psum.tile([P, 512], F32, name="rk_ps%d" % j, tag=("A", "B", "G", "X")[j], bufs=(1, 1, 2, 4)[j])
                nc.tensor.matmul(acc[:], lhsT=ones[:], rhs=rk_row[:, 512 * j:512 * j + 512], start=True, stop=True)
                nc.scalar.copy(out=rk_all[:, 512 * j:512 * j + 512], in_=acc[:])

        def turn_ln_and_g_hid():
            ln_ps = psum.tile([P, 2, P], F32, name="ln_ps", tag="B", bufs=1)
            for half in range(2):
                nc.tensor.transpose(ln_ps[:, half, :], ln_rows[:].bitcast(F32)[:, half:2 * P:2], ident[:])
            nc.vector.tensor_copy(out=ln_words[:].rearrange("p (n u) -> p n u", u=2), in_=ln_ps[:, :, 0:8].rearrange("p u n -> p n u"))
            nc.vector.tensor_copy(out=ln_cols[:], in_=ln_words[:].bitcast(BF16))
            gh_ps = psum.tile([P, 512], F32, name="gh_ps", tag="G", bufs=2)
            for m in range(TILES):
                nc.tensor.transpose(gh_ps[:, P * m:P * m + P], gh_rows[:].bitcast(F32)[:, P * m:P * m + P], ident[:])
            nc.vector.tensor_copy(out=gh_t[:], in_=gh_ps[:].bitcast(BF16).rearrange("q (n e) -> q e n", e=2))

        bn_out, std, a_b, dots, rkw = {}, {}, {}, {}, {}
        s1, s2, s1_ps, s2_ps, gate_ps, e1, z_bf, w_bf, w_ps, out_ps = {}, {}, {}, {}, {}, {}, {}, {}, {}, {}

        def bn_part(m, part):
            if part == 0:
                bn_out[m] = work.tile([P, HEADS, 3], F32, name="bn%d" % m, tag="bn")
            for pair in range(4 * part, 4 * part + 4):
                two_heads = y_sb[m][:, 2 * HEAD * pair:2 * HEAD * pair + 2 * HEAD].rearrange("t (h i) -> t i h", h=2)
                nc.vector.bn_stats(out=bn_out[m][:, 2 * pair:2 * pair + 2, :].rearrange("t h s -> t (h s)"), in_=two_heads)

        def root(m):
            std[m] = work.tile([P, HEADS], F32, name="std%d" % m, tag="std")
            nc.scalar.activation(out=std[m][:], in_=bn_out[m][:, :, 2], func=SQRT, scale=1.0 / HEAD, bias=EPS)

        def scale_and_shift(m):
            a_b[m] = work.tile([P, 2, HEADS], F32, name="ab%d" % m, tag="ab")
            nc.vector.reciprocal(out=a_b[m][:, 0, :], in_=std[m][:])
            nc.vector.scalar_tensor_tensor(out=a_b[m][:, 1, :], in0=bn_out[m][:, :, 1], scalar=-1.0, in1=a_b[m][:, 0, :],
                                           op0=MUL, op1=MUL)

        def products(m):
            rkw[m] = work.tile([P, C], F32, name="rkw%d" % m, tag="rkw")
            dots[m] = work.tile([P, HEADS], F32, name="dot%d" % m, tag="dot")
            for first in range(0, C, 2 * GW):
                both = (slice(first, first + GW), slice(first + GW, first + 2 * GW))
                for cols in both:
                    nc.gpsimd.tensor_tensor(out=rkw[m][:, cols], in0=r_sb[m][:, cols], in1=k_sb[m][:, cols], op=MUL)
                for cols in both:
                    nc.gpsimd.tensor_tensor(out=rkw[m][:, cols], in0=rkw[m][:, cols], in1=rk_all[:, cols], op=MUL)

        def dot_sum(u):
            m, g = divmod(u, PASSES)
            nc.vector.tensor_reduce(out=dots[m][:, 8 * g:8 * g + 8],
                                    in_=rkw[m][:, 512 * g:512 * g + 512].rearrange("t (h i) -> t h i", i=HEAD),
                                    axis=AXIS_X, op=ADD)

        def split_view(tile_ap, h):
            return tile_ap[:, HEAD * h:HEAD * h + HEAD].rearrange("t (p f) -> t f p", f=4)

        def norm_heads(u):
            m, g = divmod(u, PASSES)
            s1[u] = work.tile([P, 4, P], F32, name="s1_%d" % u, tag="s1", bufs=3)
            for i in range(8):
                h = 8 * g + i
                nc.scalar.activation(out=s1[u][:, :, 16 * i:16 * i + 16],
                                     in_=split_view(y_sb[m], h), func=IDENTITY,
                                     bias=a_b[m][:, 1, h:h + 1], scale=a_b[m][:, 0, h:h + 1])

        def bonus_heads(u):
            m, g = divmod(u, PASSES)
            s2[u] = work.tile([P, 4, P], F32, name="s2_%d" % u, tag="s2", bufs=3)
            for i in range(8):
                h = 8 * g + i
                nc.scalar.activation(out=s2[u][:, :, 16 * i:16 * i + 16],
                                     in_=split_view(v_sb[m], h), func=COPY, scale=dots[m][:, h:h + 1])

        def turn_s1(u):
            s1_ps[u] = psum.tile([P, 4, P], F32, name="s1ps%d" % u, tag="A", bufs=1)
            for t in range(4):
                nc.tensor.transpose(s1_ps[u][:, t, :], s1[u][:, t, :], ident[:])

        def turn_s2(u):
            s2_ps[u] = psum.tile([P, 4, P], F32, name="s2ps%d" % u, tag="B", bufs=1)
            for t in range(4):
                nc.tensor.transpose(s2_ps[u][:, t, :], s2[u][:, t, :], ident[:])

        def gate(u, slots):
            m, g = divmod(u, PASSES)
            if slots[0] == 0:
                gate_ps[u] = psum.tile([P, 4, P], F32, name="gps%d" % u, tag="G", bufs=2)
            for t in slots:
                for e in range(2):
                    every_fourth = g2_sb[:, e, 512 * g:512 * g + 512].rearrange("q (p f) -> q f p", f=4)[:, t, :]
                    nc.tensor.matmul(gate_ps[u][:, t, :], lhsT=every_fourth, rhs=gh_t[:, e, P * m:P * m + P],
                                     start=(e == 0), stop=(e == 1))

        def gain_and_bias(u):
            g = u % PASSES
            e1[u] = work.tile([P, 4, P], F32, name="e1_%d" % u, tag="e1", bufs=3)
            for t in range(4):
                blk = 4 * g + t
                nc.scalar.activation(out=e1[u][:, t, :], in_=s1_ps[u][:, t, :], func=IDENTITY,
                                     bias=ln_cols[:, 16 + blk:17 + blk], scale=ln_cols[:, blk:blk + 1])

        def add_bonus(u):
            nc.vector.tensor_tensor(out=e1[u][:], in0=e1[u][:], in1=s2_ps[u][:], op=ADD)

        def times_gate(u):
            m, g = divmod(u, PASSES)
            if g == 0:
                z_bf[m] = work.tile([P, 512, 4], BF16, name="z%d" % m, tag="z", bufs=2, align_bytes=64)
            nc.vector.tensor_tensor(out=z_bf[m][:, P * g:P * g + P, :], in0=e1[u][:].rearrange("p t r -> p r t"),
                                    in1=gate_ps[u][:].rearrange("p t r -> p r t"), op=MUL)

        def quantise_z(m, first, last):
            cols = slice(P * first, P * last + P)
            nc.vector.quantize_mx(out=z_codes[:, m, cols].bitcast(FP8X4), scales=z_scales[:, m, cols],
                                  in_=z_bf[m][:, cols, :].rearrange("p r t -> p (r t)"))

        def turn_w(w):
            q, g = divmod(w, PASSES)
            for pair in range(2):
                w_ps[(w, pair)] = psum.tile([P, 2, 256], F32, name="wps%d_%d" % (w, pair), tag="X", bufs=4)
                for dummy in range(5 if w == 0 and pair == 0 else 0):
                    nc.tensor.matmul(w_ps[(w, pair)][:].rearrange("p u c -> p (u c)"), lhsT=ones[:], rhs=rk_all[:, 0:512], start=True, stop=True)
                if pair == 0 or w < 12:
                    nc.tensor.matmul(w_ps[(w, pair)][:, 0, 0:P], lhsT=ident[:], rhs=ident[:], start=True, stop=True)
                for half in range(2):
                    for b in range(2):
                        nc.tensor.transpose(w_ps[(w, pair)][:, half, P * b:P * b + P],
                                            w_sb[(q, 2 * pair + b)][:].bitcast(F32)[:, 256 * g + half:256 * g + 256:2], ident[:])

        def regroup_w(w):
            if w % 2 == 0:
                w_bf[w // 2] = work.tile([P, 4096], BF16, name="wbf%d" % w, tag="wbf", bufs=2, align_bytes=64)
            words = w_bf[w // 2][:].bitcast(F32).rearrange("p (c u) -> p c u", u=2)
            for pair in range(2):
                first = 512 * (w % 2) + 256 * pair
                if w % 4 == 1 and pair == 1:
                    nc.vector.tensor_copy(out=words[:, first:first + 256, :], in_=w_ps[(w, pair)][:].rearrange("p u c -> p c u"))
                else:
                    nc.scalar.copy(out=words[:, first:first + 256, :], in_=w_ps[(w, pair)][:].rearrange("p u c -> p c u"))

        def quantise_w(two):
            q, half = divmod(two, 2)
            nc.vector.quantize_mx(out=w_codes[:, q, 1024 * half:1024 * half + 1024].bitcast(FP8X4),
                                  scales=w_scales[:, q, 1024 * half:1024 * half + 1024], in_=w_bf[two][:])

        def mx_pass(m, g, n):
            nc.tensor.matmul_mx(out=out_ps[(m, n)][:],
                                lhsT=z_codes[:, m, P * g:P * g + P].bitcast(FP8X4), lhsT_scale=z_scales[:, m, P * g:P * g + P],
                                rhs=w_codes[:, n, 512 * g:512 * g + 512].bitcast(FP8X4), rhs_scale=w_scales[:, n, 512 * g:512 * g + 512],
                                start=(g == 0), stop=(g == PASSES - 1))

        def open_bank(m, n):
            out_ps[(m, n)] = psum.tile([P, 512], F32, name="ops%d_%d" % (m, n), tag="X", bufs=4)

        def store(m, n, on_vector):
            res = work.tile([P, 512], F32, name="res%d_%d" % (m, n), tag="res", bufs=4)
            if on_vector:
                nc.vector.tensor_copy(out=res[:], in_=out_ps[(m, n)][:])
            else:
                nc.scalar.copy(out=res[:], in_=out_ps[(m, n)][:])
            nc.sync.dma_start(out=out[m, :, 512 * n:512 * n + 512], in_=res[:])

        def is_unit(u):
            return 0 <= u < UNITS

        def is_w_unit(w):
            return 0 <= w < W_UNITS

        def groups_of_step(s):
            if 5 <= s < 9:
                return [(0, s - 5)]
            if 9 <= s < 12:
                return [(1, 0)] if s == 9 else [(1, 1), (1, 2)] if s == 10 else [(1, 3)]
            if 12 <= s < 14:
                return [(2, 2 * (s - 12)), (2, 2 * (s - 12) + 1)]
            return []

        spread_r_k()
        for s in range(-6, UNITS + 1):
            for m in range(TILES):
                if s == 4 * m - 4:
                    root(m)
            if is_unit(s):
                add_bonus(s)
            if is_w_unit(2 * (s - 1)):
                quantise_w(s - 1)
            if is_unit(s):
                times_gate(s)
            for m in range(TILES):
                if s in (4 * m - 6, 4 * m - 5):
                    bn_part(m, 2 * (s - 4 * m + 6))
                    bn_part(m, 2 * (s - 4 * m + 6) + 1)
                if s == 4 * m - 6:
                    products(m)
            for (m, n) in groups_of_step(s - 1):
                if n % 2 == 1:
                    store(m, n, True)
            if is_unit(s + 3):
                dot_sum(s + 3)
            for m in range(TILES):
                if s == 4 * m - 4:
                    scale_and_shift(m)
            if is_unit(s):
                m, g = divmod(s, PASSES)
                if m == TILES - 1:
                    quantise_z(m, g, g)
                elif g == PASSES - 1:
                    quantise_z(m, 0, g)
            if s == -4:
                turn_ln_and_g_hid()
            for half in range(2):
                if is_w_unit(2 * s + half):
                    turn_w(2 * s + half)
                if is_unit(s + 1):
                    gate(s + 1, (2 * half, 2 * half + 1))
            if is_unit(s + 2):
                turn_s1(s + 2)
            if is_unit(s + 1):
                turn_s2(s + 1)
            for (m, n) in groups_of_step(s):
                open_bank(m, n)
                for g in range(PASSES):
                    mx_pass(m, g, n)
            for g in {14: (0, 1), 15: (2,), 16: (3,)}.get(s, ()):
                for n in range(4):
                    if g == 0:
                        open_bank(TILES - 1, n)
                    mx_pass(TILES - 1, g, n)
            for w in (2 * s, 2 * s + 1):
                if is_w_unit(w):
                    regroup_w(w)
            if is_unit(s + 3):
                norm_heads(s + 3)
            if is_unit(s + 2):
                bonus_heads(s + 2)
            for (m, n) in groups_of_step(s - 1):
                if n % 2 == 0:
                    store(m, n, False)
            if is_unit(s + 2):
                gain_and_bias(s + 2)
        for n in range(4):
            store(TILES - 1, n, n % 2 == 1)
